import numpy as np
import ml_dtypes

BF16 = ml_dtypes.bfloat16


def bf(x):
    return np.asarray(x, np.float32).astype(BF16)


def f32(x):
    return np.asarray(x, np.float32)


def f64(x):
    return np.asarray(x).astype(np.float64)


def striped(idx):
    return np.tile(idx.reshape(-1, 16).T, (8, 1))


F, S, N, M = 128, 4096, 2048, 256
ALPHA = 0.25


def prelu(v):
    return np.where(v >= 0.0, v, ALPHA * v)


def setup_inputs():
    return {
        "table": bf(np.random.standard_normal((F, S))),
        "w1": bf(np.random.standard_normal((F, M)) / np.sqrt(F)),
        "adj_t": bf(np.random.standard_normal((N, N)) / np.sqrt(N)),
        "b1": f32(0.1 * np.random.standard_normal((M, 1))),
        "w2": bf(np.random.standard_normal((M, M)) * np.sqrt(2.0 / M)),
        "b2": f32(0.1 * np.random.standard_normal((M, 1))),
        "w3": bf(np.random.standard_normal((M, M)) * np.sqrt(2.0 / M)),
        "b3": f32(0.1 * np.random.standard_normal((M, 1))),
        "offs": striped(np.random.permutation(S)[:N]),
    }


def reference(table, w1, adj_t, b1, w2, b2, w3, b3, offs):
    idx = offs[:16].T.reshape(-1)
    a = f64(adj_t)
    u1 = f64(w1).T @ f64(table)[:, idx]
    h1 = prelu(u1 @ a + f64(b1))
    u2 = f64(w2).T @ h1
    h2 = prelu(u2 @ a + f64(b2))
    u3 = f64(w3).T @ h2
    h3 = prelu(u3 @ a + f64(b3))
    return np.concatenate([h1, h2, h3], axis=0)

@@ -1,0 +1,125 @@
+import concourse.mybir as mybir
+from concourse.masks import make_identity
+
+BF16, F32, U16 = mybir.dt.bfloat16, mybir.dt.float32, mybir.dt.uint16
+IDENTITY = mybir.ActivationFunctionType.Identity
+MULT, MAX = mybir.AluOpType.mult, mybir.AluOpType.max
+
+P = 128
+F, S, N, M = 128, 4096, 2048, 256
+LAYERS = 3
+ALPHA = 0.25
+PIECE = 512
+N_PIECES = N // PIECE
+N_JB = N // P
+JB_IN_PIECE = PIECE // P
+N_MB = M // P
+
+FLOPS = 2 * F * M * N + LAYERS * 2 * M * N * N + (LAYERS - 1) * 2 * M * M * N
+
+
+def tile_mvrl_gcn_b_kernel(tc, table, w1, adj_t, b1, w2, b2, w3, b3, offs, out):
+    nc = tc.nc
+    with (
+        tc.tile_pool(name="held", bufs=1) as held,
+        tc.tile_pool(name="layer", bufs=2) as layer_pool,
+        tc.tile_pool(name="stage", bufs=4) as stage,
+        tc.psum_pool(name="psum_acc", bufs=4) as psum_acc,
+        tc.psum_pool(name="psum_u", bufs=4) as psum_u,
+    ):
+        offsets = held.tile([P, N // 16], U16, name="offsets")
+        nc.sync.dma_start(offsets[:], offs)
+        table_sb = held.tile([P, S], BF16, name="table_sb")
+        nc.sync.dma_start(table_sb[:], table)
+        w1_sb = held.tile([P, M], BF16, name="w1_sb")
+        nc.scalar.dma_start(w1_sb[:], w1)
+
+        adj_blocks = adj_t.rearrange("(jb j) i -> j jb i", j=P)
+        adj_sb = []
+        for p in range(N_PIECES):
+            adj_piece = held.tile([P, N_JB, PIECE], BF16, name=f"adj{p}")
+            nc.sync.dma_start(adj_piece[:], adj_blocks[:, :, p * PIECE : (p + 1) * PIECE])
+            adj_sb.append(adj_piece)
+
+        w_sb = {}
+        for l, w in ((1, w2), (2, w3)):
+            w_sb[l] = held.tile([P, N_MB, M], BF16, name=f"w_sb{l}")
+            nc.scalar.dma_start(w_sb[l][:], w.rearrange("(fb f) m -> f fb m", f=P))
+
+        bias_sb = []
+        with nc.allow_non_contiguous_dma(reason="a bias of 256 floats, one element to a partition"):
+            for l, b in enumerate((b1, b2, b3)):
+                bias = held.tile([P, N_MB, 1], F32, name=f"bias{l}")
+                nc.scalar.dma_start(bias[:], b.rearrange("(mb m) one -> m mb one", m=P))
+                bias_sb.append(bias)
+
+        identity = held.tile([P, P], BF16, name="identity")
+        make_identity(nc, identity[:])
+
+        u1_bf = held.tile([P, N_MB, N], BF16, name="u1_bf")
+        for q in range(N_PIECES):
+            piece_offsets = offsets[:, q * (PIECE // 16) : (q + 1) * (PIECE // 16)]
+            for mb in range(N_MB):
+                u1_ps = psum_u.tile([P, PIECE], F32, tag="u")
+                nc.tensor.matmul(
+                    u1_ps[:],
+                    w1_sb[:, mb * P : (mb + 1) * P],
+                    table_sb[:].indirect(piece_offsets),
+                    start=True,
+                    stop=True,
+                )
+                nc.vector.tensor_copy(u1_bf[:, mb, q * PIECE : (q + 1) * PIECE], u1_ps[:])
+
+        uT = layer_pool.tile([P, N_JB, M], BF16, name="uT")
+        for q in range(N_PIECES):
+            flipped = psum_u.tile([P, JB_IN_PIECE, M], BF16, tag="u")
+            for k in range(JB_IN_PIECE):
+                jb = q * JB_IN_PIECE + k
+                for mb in range(N_MB):
+                    nc.tensor.transpose(
+                        flipped[:, k, mb * P : (mb + 1) * P],
+                        u1_bf[:, mb, jb * P : (jb + 1) * P],
+                        identity[:],
+                    )
+            nc.vector.tensor_copy(uT[:, q * JB_IN_PIECE : (q + 1) * JB_IN_PIECE, :], flipped[:])
+
+        for l in range(LAYERS):
+            last = l == LAYERS - 1
+            if not last:
+                h_bf = layer_pool.tile([P, N_MB, N], BF16, name="h_bf")
+            for p in range(N_PIECES):
+                columns = slice(p * PIECE, (p + 1) * PIECE)
+                for mb in range(N_MB):
+                    acc = psum_acc.tile([P, PIECE], F32, name="acc")
+                    for jb in range(N_JB):
+                        nc.tensor.matmul(
+                            acc[:],
+                            uT[:, jb, mb * P : (mb + 1) * P],
+                            adj_sb[p][:, jb, :],
+                            start=(jb == 0),
+                            stop=(jb == N_JB - 1),
+                        )
+                    biased = stage.tile([P, PIECE], F32, name="biased")
+                    nc.scalar.activation(biased[:], acc[:], IDENTITY, bias=bias_sb[l][:, mb, :])
+                    h = stage.tile([P, PIECE], F32, name="h")
+                    nc.vector.scalar_tensor_tensor(h[:], biased[:], ALPHA, biased[:], op0=MULT, op1=MAX)
+                    if not last:
+                        nc.vector.tensor_copy(h_bf[:, mb, columns], h[:])
+                    rows = slice(l * M + mb * P, l * M + (mb + 1) * P)
+                    nc.sync.dma_start(out[rows, columns], h[:])
+
+            if not last:
+                uT = layer_pool.tile([P, N_JB, M], BF16, name="uT")
+                for jb0 in range(0, N_JB, 2):
+                    u_ps = psum_u.tile([P, 2, M], F32, tag="u")
+                    for k in range(2):
+                        jb = jb0 + k
+                        for fb in range(N_MB):
+                            nc.tensor.matmul(
+                                u_ps[:, k, :],
+                                h_bf[:, fb, jb * P : (jb + 1) * P],
+                                w_sb[l + 1][:, fb, :],
+                                start=(fb == 0),
+                                stop=(fb == N_MB - 1),
+                            )
+                    nc.vector.tensor_copy(uT[:, jb0 : jb0 + 2, :], u_ps[:])

@@ -76,10 +76,12 @@ def tile_mvrl_gcn_b_kernel(tc, table, w1, adj_t, b1, w2, b2, w3, b3, offs, out):
             for k in range(JB_IN_PIECE):
                 jb = q * JB_IN_PIECE + k
                 for mb in range(N_MB):
-                    nc.tensor.transpose(
+                    nc.tensor.matmul(
                         flipped[:, k, mb * P : (mb + 1) * P],
                         u1_bf[:, mb, jb * P : (jb + 1) * P],
                         identity[:],
+                        start=True,
+                        stop=True,
                     )
             nc.vector.tensor_copy(uT[:, q * JB_IN_PIECE : (q + 1) * JB_IN_PIECE, :], flipped[:])
 

@@ -14,6 +14,7 @@ N_PIECES = N // PIECE
 N_JB = N // P
 JB_IN_PIECE = PIECE // P
 N_MB = M // P
+WARM_UP_MATMULS = 24
 
 FLOPS = 2 * F * M * N + LAYERS * 2 * M * N * N + (LAYERS - 1) * 2 * M * M * N
 
@@ -56,6 +57,10 @@ def tile_mvrl_gcn_b_kernel(tc, table, w1, adj_t, b1, w2, b2, w3, b3, offs, out):
         identity = held.tile([P, P], BF16, name="identity")
         make_identity(nc, identity[:])
 
+        warm_ps = psum_u.tile([P, P], F32, tag="u")
+        for i in range(WARM_UP_MATMULS):
+            nc.tensor.matmul(warm_ps[:], identity[:], identity[:], start=True, stop=True)
+
         u1_bf = held.tile([P, N_MB, N], BF16, name="u1_bf")
         for q in range(N_PIECES):
             piece_offsets = offsets[:, q * (PIECE // 16) : (q + 1) * (PIECE // 16)]
@@ -76,12 +81,10 @@ def tile_mvrl_gcn_b_kernel(tc, table, w1, adj_t, b1, w2, b2, w3, b3, offs, out):
             for k in range(JB_IN_PIECE):
                 jb = q * JB_IN_PIECE + k
                 for mb in range(N_MB):
-                    nc.tensor.matmul(
+                    nc.tensor.transpose(
                         flipped[:, k, mb * P : (mb + 1) * P],
                         u1_bf[:, mb, jb * P : (jb + 1) * P],
                         identity[:],
-                        start=True,
-                        stop=True,
                     )
             nc.vector.tensor_copy(uT[:, q * JB_IN_PIECE : (q + 1) * JB_IN_PIECE, :], flipped[:])
 

@@ -14,7 +14,7 @@ N_PIECES = N // PIECE
 N_JB = N // P
 JB_IN_PIECE = PIECE // P
 N_MB = M // P
-WARM_UP_MATMULS = 24
+JB_IN_LOAD = 4
 
 FLOPS = 2 * F * M * N + LAYERS * 2 * M * N * N + (LAYERS - 1) * 2 * M * M * N
 
@@ -36,30 +36,32 @@ def tile_mvrl_gcn_b_kernel(tc, table, w1, adj_t, b1, w2, b2, w3, b3, offs, out):
         nc.scalar.dma_start(w1_sb[:], w1)
 
         adj_blocks = adj_t.rearrange("(jb j) i -> j jb i", j=P)
-        adj_sb = []
-        for p in range(N_PIECES):
-            adj_piece = held.tile([P, N_JB, PIECE], BF16, name=f"adj{p}")
-            nc.sync.dma_start(adj_piece[:], adj_blocks[:, :, p * PIECE : (p + 1) * PIECE])
-            adj_sb.append(adj_piece)
+        adj_sb = [held.tile([P, N_JB, PIECE], BF16, name=f"adj{p}") for p in range(N_PIECES)]
 
-        w_sb = {}
-        for l, w in ((1, w2), (2, w3)):
-            w_sb[l] = held.tile([P, N_MB, M], BF16, name=f"w_sb{l}")
-            nc.scalar.dma_start(w_sb[l][:], w.rearrange("(fb f) m -> f fb m", f=P))
+        def load_adj_piece(p):
+            for jb0 in range(0, N_JB, JB_IN_LOAD):
+                senders = slice(jb0, jb0 + JB_IN_LOAD)
+                nc.sync.dma_start(adj_sb[p][:, senders, :], adj_blocks[:, senders, p * PIECE : (p + 1) * PIECE])
+
+        load_adj_piece(0)
 
         bias_sb = []
         with nc.allow_non_contiguous_dma(reason="a bias of 256 floats, one element to a partition"):
             for l, b in enumerate((b1, b2, b3)):
                 bias = held.tile([P, N_MB, 1], F32, name=f"bias{l}")
-                nc.scalar.dma_start(bias[:], b.rearrange("(mb m) one -> m mb one", m=P))
+                nc.sync.dma_start(bias[:], b.rearrange("(mb m) one -> m mb one", m=P))
                 bias_sb.append(bias)
+
+        for p in range(1, N_PIECES):
+            load_adj_piece(p)
+
+        w_sb = {}
+        for l, w in ((1, w2), (2, w3)):
+            w_sb[l] = held.tile([P, N_MB, M], BF16, name=f"w_sb{l}")
+            nc.sync.dma_start(w_sb[l][:], w.rearrange("(fb f) m -> f fb m", f=P))
 
         identity = held.tile([P, P], BF16, name="identity")
         make_identity(nc, identity[:])
-
-        warm_ps = psum_u.tile([P, P], F32, tag="u")
-        for i in range(WARM_UP_MATMULS):
-            nc.tensor.matmul(warm_ps[:], identity[:], identity[:], start=True, stop=True)
 
         u1_bf = held.tile([P, N_MB, N], BF16, name="u1_bf")
         for q in range(N_PIECES):

@@ -15,6 +15,7 @@ N_JB = N // P
 JB_IN_PIECE = PIECE // P
 N_MB = M // P
 JB_IN_LOAD = 4
+TAIL_WIDTH = 128
 
 FLOPS = 2 * F * M * N + LAYERS * 2 * M * N * N + (LAYERS - 1) * 2 * M * M * N
 
@@ -95,25 +96,28 @@ def tile_mvrl_gcn_b_kernel(tc, table, w1, adj_t, b1, w2, b2, w3, b3, offs, out):
             if not last:
                 h_bf = layer_pool.tile([P, N_MB, N], BF16, name="h_bf")
             for p in range(N_PIECES):
-                columns = slice(p * PIECE, (p + 1) * PIECE)
                 for mb in range(N_MB):
-                    acc = psum_acc.tile([P, PIECE], F32, name="acc")
-                    for jb in range(N_JB):
-                        nc.tensor.matmul(
-                            acc[:],
-                            uT[:, jb, mb * P : (mb + 1) * P],
-                            adj_sb[p][:, jb, :],
-                            start=(jb == 0),
-                            stop=(jb == N_JB - 1),
-                        )
-                    biased = stage.tile([P, PIECE], F32, name="biased")
-                    nc.scalar.activation(biased[:], acc[:], IDENTITY, bias=bias_sb[l][:, mb, :])
-                    h = stage.tile([P, PIECE], F32, name="h")
-                    nc.vector.scalar_tensor_tensor(h[:], biased[:], ALPHA, biased[:], op0=MULT, op1=MAX)
-                    if not last:
-                        nc.vector.tensor_copy(h_bf[:, mb, columns], h[:])
-                    rows = slice(l * M + mb * P, l * M + (mb + 1) * P)
-                    nc.sync.dma_start(out[rows, columns], h[:])
+                    final = last and p == N_PIECES - 1 and mb == N_MB - 1
+                    width = TAIL_WIDTH if final else PIECE
+                    for c0 in range(0, PIECE, width):
+                        columns = slice(p * PIECE + c0, p * PIECE + c0 + width)
+                        acc = psum_acc.tile([P, width], F32, tag="acc")
+                        for jb in range(N_JB):
+                            nc.tensor.matmul(
+                                acc[:],
+                                uT[:, jb, mb * P : (mb + 1) * P],
+                                adj_sb[p][:, jb, c0 : c0 + width],
+                                start=(jb == 0),
+                                stop=(jb == N_JB - 1),
+                            )
+                        biased = stage.tile([P, width], F32, tag="biased")
+                        nc.scalar.activation(biased[:], acc[:], IDENTITY, bias=bias_sb[l][:, mb, :])
+                        h = stage.tile([P, width], F32, tag="h")
+                        nc.vector.scalar_tensor_tensor(h[:], biased[:], ALPHA, biased[:], op0=MULT, op1=MAX)
+                        if not last:
+                            nc.vector.tensor_copy(h_bf[:, mb, columns], h[:])
+                        rows = slice(l * M + mb * P, l * M + (mb + 1) * P)
+                        nc.sync.dma_start(out[rows, columns], h[:])
 
             if not last:
                 uT = layer_pool.tile([P, N_JB, M], BF16, name="uT")

@@ -15,6 +15,7 @@ N_JB = N // P
 JB_IN_PIECE = PIECE // P
 N_MB = M // P
 JB_IN_LOAD = 4
+UNITS_AHEAD = 2
 TAIL_WIDTH = 128
 
 FLOPS = 2 * F * M * N + LAYERS * 2 * M * N * N + (LAYERS - 1) * 2 * M * M * N
@@ -65,31 +66,35 @@ def tile_mvrl_gcn_b_kernel(tc, table, w1, adj_t, b1, w2, b2, w3, b3, offs, out):
         make_identity(nc, identity[:])
 
         u1_bf = held.tile([P, N_MB, N], BF16, name="u1_bf")
-        for q in range(N_PIECES):
-            piece_offsets = offsets[:, q * (PIECE // 16) : (q + 1) * (PIECE // 16)]
-            for mb in range(N_MB):
+        for mb in range(N_MB):
+            for q in range(N_PIECES):
                 u1_ps = psum_u.tile([P, PIECE], F32, tag="u")
                 nc.tensor.matmul(
                     u1_ps[:],
                     w1_sb[:, mb * P : (mb + 1) * P],
-                    table_sb[:].indirect(piece_offsets),
+                    table_sb[:].indirect(offsets[:, q * (PIECE // 16) : (q + 1) * (PIECE // 16)]),
                     start=True,
                     stop=True,
                 )
                 nc.vector.tensor_copy(u1_bf[:, mb, q * PIECE : (q + 1) * PIECE], u1_ps[:])
 
         uT = layer_pool.tile([P, N_JB, M], BF16, name="uT")
-        for q in range(N_PIECES):
-            flipped = psum_u.tile([P, JB_IN_PIECE, M], BF16, tag="u")
+        units = [(mb, q) for mb in range(N_MB) for q in range(N_PIECES)]
+        flipped = {}
+
+        def flip_block(n, k):
+            mb, q = units[n]
+            if k == 0:
+                flipped[n] = psum_u.tile([P, JB_IN_PIECE, P], BF16, tag="u", name=f"flipped{n}")
+            jb = q * JB_IN_PIECE + k
+            nc.tensor.transpose(flipped[n][:, k, :], u1_bf[:, mb, jb * P : (jb + 1) * P], identity[:])
+            if k == JB_IN_PIECE - 1:
+                senders = slice(q * JB_IN_PIECE, (q + 1) * JB_IN_PIECE)
+                nc.vector.tensor_copy(uT[:, senders, mb * P : (mb + 1) * P], flipped[n][:])
+
+        for n in range(UNITS_AHEAD):
             for k in range(JB_IN_PIECE):
-                jb = q * JB_IN_PIECE + k
-                for mb in range(N_MB):
-                    nc.tensor.transpose(
-                        flipped[:, k, mb * P : (mb + 1) * P],
-                        u1_bf[:, mb, jb * P : (jb + 1) * P],
-                        identity[:],
-                    )
-            nc.vector.tensor_copy(uT[:, q * JB_IN_PIECE : (q + 1) * JB_IN_PIECE, :], flipped[:])
+                flip_block(n, k)
 
         for l in range(LAYERS):
             last = l == LAYERS - 1
@@ -110,6 +115,10 @@ def tile_mvrl_gcn_b_kernel(tc, table, w1, adj_t, b1, w2, b2, w3, b3, offs, out):
                                 start=(jb == 0),
                                 stop=(jb == N_JB - 1),
                             )
+                            if l == 0 and p == 0:
+                                n = mb * N_PIECES + jb // JB_IN_PIECE + UNITS_AHEAD
+                                if n < len(units):
+                                    flip_block(n, jb % JB_IN_PIECE)
                         biased = stage.tile([P, width], F32, tag="biased")
                         nc.scalar.activation(biased[:], acc[:], IDENTITY, bias=bias_sb[l][:, mb, :])
                         h = stage.tile([P, width], F32, tag="h")

@@ -15,7 +15,7 @@ N_JB = N // P
 JB_IN_PIECE = PIECE // P
 N_MB = M // P
 JB_IN_LOAD = 4
-UNITS_AHEAD = 2
+FLIP_LAG = 2
 TAIL_WIDTH = 128
 
 FLOPS = 2 * F * M * N + LAYERS * 2 * M * N * N + (LAYERS - 1) * 2 * M * M * N
@@ -27,8 +27,7 @@ def tile_mvrl_gcn_b_kernel(tc, table, w1, adj_t, b1, w2, b2, w3, b3, offs, out):
         tc.tile_pool(name="held", bufs=1) as held,
         tc.tile_pool(name="layer", bufs=2) as layer_pool,
         tc.tile_pool(name="stage", bufs=4) as stage,
-        tc.psum_pool(name="psum_acc", bufs=4) as psum_acc,
-        tc.psum_pool(name="psum_u", bufs=4) as psum_u,
+        tc.psum_pool(name="psum", bufs=8) as psum,
     ):
         offsets = held.tile([P, N // 16], U16, name="offsets")
         nc.sync.dma_start(offsets[:], offs)
@@ -65,36 +64,38 @@ def tile_mvrl_gcn_b_kernel(tc, table, w1, adj_t, b1, w2, b2, w3, b3, offs, out):
         identity = held.tile([P, P], BF16, name="identity")
         make_identity(nc, identity[:])
 
-        u1_bf = held.tile([P, N_MB, N], BF16, name="u1_bf")
-        for mb in range(N_MB):
-            for q in range(N_PIECES):
-                u1_ps = psum_u.tile([P, PIECE], F32, tag="u")
-                nc.tensor.matmul(
-                    u1_ps[:],
-                    w1_sb[:, mb * P : (mb + 1) * P],
-                    table_sb[:].indirect(offsets[:, q * (PIECE // 16) : (q + 1) * (PIECE // 16)]),
-                    start=True,
-                    stop=True,
-                )
-                nc.vector.tensor_copy(u1_bf[:, mb, q * PIECE : (q + 1) * PIECE], u1_ps[:])
-
-        uT = layer_pool.tile([P, N_JB, M], BF16, name="uT")
         units = [(mb, q) for mb in range(N_MB) for q in range(N_PIECES)]
+        u1_bf = held.tile([P, N_MB, N], BF16, name="u1_bf")
+        uT = layer_pool.tile([P, N_JB, M], BF16, name="uT")
         flipped = {}
+
+        def gather_unit(n):
+            mb, q = units[n]
+            u1_ps = psum.tile([P, PIECE], F32, tag="bank")
+            nc.tensor.matmul(
+                u1_ps[:],
+                w1_sb[:, mb * P : (mb + 1) * P],
+                table_sb[:].indirect(offsets[:, q * (PIECE // 16) : (q + 1) * (PIECE // 16)]),
+                start=True,
+                stop=True,
+            )
+            nc.scalar.copy(u1_bf[:, mb, q * PIECE : (q + 1) * PIECE], u1_ps[:])
 
         def flip_block(n, k):
             mb, q = units[n]
             if k == 0:
-                flipped[n] = psum_u.tile([P, JB_IN_PIECE, P], BF16, tag="u", name=f"flipped{n}")
+                flipped[n] = psum.tile([P, JB_IN_PIECE, P], BF16, tag="bank", name=f"flipped{n}")
             jb = q * JB_IN_PIECE + k
             nc.tensor.transpose(flipped[n][:, k, :], u1_bf[:, mb, jb * P : (jb + 1) * P], identity[:])
             if k == JB_IN_PIECE - 1:
                 senders = slice(q * JB_IN_PIECE, (q + 1) * JB_IN_PIECE)
                 nc.vector.tensor_copy(uT[:, senders, mb * P : (mb + 1) * P], flipped[n][:])
 
-        for n in range(UNITS_AHEAD):
-            for k in range(JB_IN_PIECE):
-                flip_block(n, k)
+        for n in range(len(units)):
+            gather_unit(n)
+            if n >= FLIP_LAG:
+                for k in range(JB_IN_PIECE):
+                    flip_block(n - FLIP_LAG, k)
 
         for l in range(LAYERS):
             last = l == LAYERS - 1
@@ -106,7 +107,7 @@ def tile_mvrl_gcn_b_kernel(tc, table, w1, adj_t, b1, w2, b2, w3, b3, offs, out):
                     width = TAIL_WIDTH if final else PIECE
                     for c0 in range(0, PIECE, width):
                         columns = slice(p * PIECE + c0, p * PIECE + c0 + width)
-                        acc = psum_acc.tile([P, width], F32, tag="acc")
+                        acc = psum.tile([P, width], F32, tag="bank")
                         for jb in range(N_JB):
                             nc.tensor.matmul(
                                 acc[:],
@@ -115,10 +116,8 @@ def tile_mvrl_gcn_b_kernel(tc, table, w1, adj_t, b1, w2, b2, w3, b3, offs, out):
                                 start=(jb == 0),
                                 stop=(jb == N_JB - 1),
                             )
-                            if l == 0 and p == 0:
-                                n = mb * N_PIECES + jb // JB_IN_PIECE + UNITS_AHEAD
-                                if n < len(units):
-                                    flip_block(n, jb % JB_IN_PIECE)
+                            if l == 0 and p == 0 and mb == 0 and jb < FLIP_LAG * JB_IN_PIECE:
+                                flip_block(len(units) - FLIP_LAG + jb // JB_IN_PIECE, jb % JB_IN_PIECE)
                         biased = stage.tile([P, width], F32, tag="biased")
                         nc.scalar.activation(biased[:], acc[:], IDENTITY, bias=bias_sb[l][:, mb, :])
                         h = stage.tile([P, width], F32, tag="h")
@@ -131,7 +130,7 @@ def tile_mvrl_gcn_b_kernel(tc, table, w1, adj_t, b1, w2, b2, w3, b3, offs, out):
             if not last:
                 uT = layer_pool.tile([P, N_JB, M], BF16, name="uT")
                 for jb0 in range(0, N_JB, 2):
-                    u_ps = psum_u.tile([P, 2, M], F32, tag="u")
+                    u_ps = psum.tile([P, 2, M], F32, tag="bank")
                     for k in range(2):
                         jb = jb0 + k
                         for fb in range(N_MB):

@@ -15,7 +15,7 @@ N_JB = N // P
 JB_IN_PIECE = PIECE // P
 N_MB = M // P
 JB_IN_LOAD = 4
-FLIP_LAG = 2
+FLIP_LAG = 4
 TAIL_WIDTH = 128
 
 FLOPS = 2 * F * M * N + LAYERS * 2 * M * N * N + (LAYERS - 1) * 2 * M * M * N

@@ -141,4 +141,7 @@ def tile_mvrl_gcn_b_kernel(tc, table, w1, adj_t, b1, w2, b2, w3, b3, offs, out):
                                 start=(fb == 0),
                                 stop=(fb == N_MB - 1),
                             )
-                    nc.vector.tensor_copy(uT[:, jb0 : jb0 + 2, :], u_ps[:])
+                    if (jb0 // 2) % 2 == 0:
+                        nc.vector.tensor_copy(uT[:, jb0 : jb0 + 2, :], u_ps[:])
+                    else:
+                        nc.scalar.copy(uT[:, jb0 : jb0 + 2, :], u_ps[:])

@@ -44,22 +44,22 @@ def tile_mvrl_gcn_b_kernel(tc, table, w1, adj_t, b1, w2, b2, w3, b3, offs, out):
                 senders = slice(jb0, jb0 + JB_IN_LOAD)
                 nc.sync.dma_start(adj_sb[p][:, senders, :], adj_blocks[:, senders, p * PIECE : (p + 1) * PIECE])
 
+        bias_sb = [held.tile([P, N_MB, 1], F32, name=f"bias{l}") for l in range(LAYERS)]
+
+        def load_bias(l, b):
+            with nc.allow_non_contiguous_dma(reason="a bias of 256 floats, one element to a partition"):
+                nc.sync.dma_start(bias_sb[l][:], b.rearrange("(mb m) one -> m mb one", m=P))
+
         load_adj_piece(0)
-
-        bias_sb = []
-        with nc.allow_non_contiguous_dma(reason="a bias of 256 floats, one element to a partition"):
-            for l, b in enumerate((b1, b2, b3)):
-                bias = held.tile([P, N_MB, 1], F32, name=f"bias{l}")
-                nc.sync.dma_start(bias[:], b.rearrange("(mb m) one -> m mb one", m=P))
-                bias_sb.append(bias)
-
+        load_bias(0, b1)
         for p in range(1, N_PIECES):
             load_adj_piece(p)
 
         w_sb = {}
-        for l, w in ((1, w2), (2, w3)):
+        for l, w, b in ((1, w2, b2), (2, w3, b3)):
             w_sb[l] = held.tile([P, N_MB, M], BF16, name=f"w_sb{l}")
             nc.sync.dma_start(w_sb[l][:], w.rearrange("(fb f) m -> f fb m", f=P))
+            load_bias(l, b)
 
         identity = held.tile([P, P], BF16, name="identity")
         make_identity(nc, identity[:])

@@ -16,7 +16,7 @@ JB_IN_PIECE = PIECE // P
 N_MB = M // P
 JB_IN_LOAD = 4
 FLIP_LAG = 4
-TAIL_WIDTH = 128
+TAIL_WIDTH = 64
 
 FLOPS = 2 * F * M * N + LAYERS * 2 * M * N * N + (LAYERS - 1) * 2 * M * M * N
 
@@ -104,8 +104,9 @@ def tile_mvrl_gcn_b_kernel(tc, table, w1, adj_t, b1, w2, b2, w3, b3, offs, out):
             for p in range(N_PIECES):
                 for mb in range(N_MB):
                     final = last and p == N_PIECES - 1 and mb == N_MB - 1
-                    width = TAIL_WIDTH if final else PIECE
-                    for c0 in range(0, PIECE, width):
+                    c0 = 0
+                    while c0 < PIECE:
+                        width = max((PIECE - c0) // 2, TAIL_WIDTH) if final else PIECE
                         columns = slice(p * PIECE + c0, p * PIECE + c0 + width)
                         acc = psum.tile([P, width], F32, tag="bank")
                         for jb in range(N_JB):
@@ -126,6 +127,7 @@ def tile_mvrl_gcn_b_kernel(tc, table, w1, adj_t, b1, w2, b2, w3, b3, offs, out):
                             nc.vector.tensor_copy(h_bf[:, mb, columns], h[:])
                         rows = slice(l * M + mb * P, l * M + (mb + 1) * P)
                         nc.sync.dma_start(out[rows, columns], h[:])
+                        c0 += width
 
             if not last:
                 uT = layer_pool.tile([P, N_JB, M], BF16, name="uT")

@@ -121,10 +121,12 @@ def tile_mvrl_gcn_b_kernel(tc, table, w1, adj_t, b1, w2, b2, w3, b3, offs, out):
                                 flip_block(len(units) - FLIP_LAG + jb // JB_IN_PIECE, jb % JB_IN_PIECE)
                         biased = stage.tile([P, width], F32, tag="biased")
                         nc.scalar.activation(biased[:], acc[:], IDENTITY, bias=bias_sb[l][:, mb, :])
+                        if not last:
+                            nc.vector.scalar_tensor_tensor(
+                                h_bf[:, mb, columns], biased[:], ALPHA, biased[:], op0=MULT, op1=MAX
+                            )
                         h = stage.tile([P, width], F32, tag="h")
                         nc.vector.scalar_tensor_tensor(h[:], biased[:], ALPHA, biased[:], op0=MULT, op1=MAX)
-                        if not last:
-                            nc.vector.tensor_copy(h_bf[:, mb, columns], h[:])
                         rows = slice(l * M + mb * P, l * M + (mb + 1) * P)
                         nc.sync.dma_start(out[rows, columns], h[:])
                         c0 += width

@@ -15,7 +15,7 @@ N_JB = N // P
 JB_IN_PIECE = PIECE // P
 N_MB = M // P
 JB_IN_LOAD = 4
-FLIP_LAG = 4
+FLIP_LAG = 5
 TAIL_WIDTH = 64
 
 FLOPS = 2 * F * M * N + LAYERS * 2 * M * N * N + (LAYERS - 1) * 2 * M * M * N
@@ -117,8 +117,9 @@ def tile_mvrl_gcn_b_kernel(tc, table, w1, adj_t, b1, w2, b2, w3, b3, offs, out):
                                 start=(jb == 0),
                                 stop=(jb == N_JB - 1),
                             )
-                            if l == 0 and p == 0 and mb == 0 and jb < FLIP_LAG * JB_IN_PIECE:
-                                flip_block(len(units) - FLIP_LAG + jb // JB_IN_PIECE, jb % JB_IN_PIECE)
+                            flip = mb * N_JB + jb
+                            if l == 0 and p == 0 and flip < FLIP_LAG * JB_IN_PIECE:
+                                flip_block(len(units) - FLIP_LAG + flip // JB_IN_PIECE, flip % JB_IN_PIECE)
                         biased = stage.tile([P, width], F32, tag="biased")
                         nc.scalar.activation(biased[:], acc[:], IDENTITY, bias=bias_sb[l][:, mb, :])
                         if not last:

import concourse.mybir as mybir
from concourse.masks import make_identity

BF16, F32, U16 = mybir.dt.bfloat16, mybir.dt.float32, mybir.dt.uint16
IDENTITY = mybir.ActivationFunctionType.Identity
MULT, MAX = mybir.AluOpType.mult, mybir.AluOpType.max

P = 128
F, S, N, M = 128, 4096, 2048, 256
LAYERS = 3
ALPHA = 0.25
PIECE = 512
N_PIECES = N // PIECE
N_JB = N // P
JB_IN_PIECE = PIECE // P
N_MB = M // P
JB_IN_LOAD = 4
FLIP_LAG = 5
TAIL_WIDTH = 64

FLOPS = 2 * F * M * N + LAYERS * 2 * M * N * N + (LAYERS - 1) * 2 * M * M * N


def tile_mvrl_gcn_b_kernel(tc, table, w1, adj_t, b1, w2, b2, w3, b3, offs, out):
    nc = tc.nc
    with (
        tc.tile_pool(name="held", bufs=1) as held,
        tc.tile_pool(name="layer", bufs=2) as layer_pool,
        tc.tile_pool(name="stage", bufs=4) as stage,
        tc.psum_pool(name="psum", bufs=8) as psum,
    ):
        offsets = held.tile([P, N // 16], U16, name="offsets")
        nc.sync.dma_start(offsets[:], offs)
        table_sb = held.tile([P, S], BF16, name="table_sb")
        nc.sync.dma_start(table_sb[:], table)
        w1_sb = held.tile([P, M], BF16, name="w1_sb")
        nc.scalar.dma_start(w1_sb[:], w1)

        adj_blocks = adj_t.rearrange("(jb j) i -> j jb i", j=P)
        adj_sb = [held.tile([P, N_JB, PIECE], BF16, name=f"adj{p}") for p in range(N_PIECES)]

        def load_adj_piece(p):
            for jb0 in range(0, N_JB, JB_IN_LOAD):
                senders = slice(jb0, jb0 + JB_IN_LOAD)
                nc.sync.dma_start(adj_sb[p][:, senders, :], adj_blocks[:, senders, p * PIECE : (p + 1) * PIECE])

        bias_sb = [held.tile([P, N_MB, 1], F32, name=f"bias{l}") for l in range(LAYERS)]

        def load_bias(l, b):
            with nc.allow_non_contiguous_dma(reason="a bias of 256 floats, one element to a partition"):
                nc.sync.dma_start(bias_sb[l][:], b.rearrange("(mb m) one -> m mb one", m=P))

        load_adj_piece(0)
        load_bias(0, b1)
        for p in range(1, N_PIECES):
            load_adj_piece(p)

        w_sb = {}
        for l, w, b in ((1, w2, b2), (2, w3, b3)):
            w_sb[l] = held.tile([P, N_MB, M], BF16, name=f"w_sb{l}")
            nc.sync.dma_start(w_sb[l][:], w.rearrange("(fb f) m -> f fb m", f=P))
            load_bias(l, b)

        identity = held.tile([P, P], BF16, name="identity")
        make_identity(nc, identity[:])

        units = [(mb, q) for mb in range(N_MB) for q in range(N_PIECES)]
        u1_bf = held.tile([P, N_MB, N], BF16, name="u1_bf")
        uT = layer_pool.tile([P, N_JB, M], BF16, name="uT")
        flipped = {}

        def gather_unit(n):
            mb, q = units[n]
            u1_ps = psum.tile([P, PIECE], F32, tag="bank")
            nc.tensor.matmul(
                u1_ps[:],
                w1_sb[:, mb * P : (mb + 1) * P],
                table_sb[:].indirect(offsets[:, q * (PIECE // 16) : (q + 1) * (PIECE // 16)]),
                start=True,
                stop=True,
            )
            nc.scalar.copy(u1_bf[:, mb, q * PIECE : (q + 1) * PIECE], u1_ps[:])

        def flip_block(n, k):
            mb, q = units[n]
            if k == 0:
                flipped[n] = psum.tile([P, JB_IN_PIECE, P], BF16, tag="bank", name=f"flipped{n}")
            jb = q * JB_IN_PIECE + k
            nc.tensor.transpose(flipped[n][:, k, :], u1_bf[:, mb, jb * P : (jb + 1) * P], identity[:])
            if k == JB_IN_PIECE - 1:
                senders = slice(q * JB_IN_PIECE, (q + 1) * JB_IN_PIECE)
                nc.vector.tensor_copy(uT[:, senders, mb * P : (mb + 1) * P], flipped[n][:])

        for n in range(len(units)):
            gather_unit(n)
            if n >= FLIP_LAG:
                for k in range(JB_IN_PIECE):
                    flip_block(n - FLIP_LAG, k)

        for l in range(LAYERS):
            last = l == LAYERS - 1
            if not last:
                h_bf = layer_pool.tile([P, N_MB, N], BF16, name="h_bf")
            for p in range(N_PIECES):
                for mb in range(N_MB):
                    final = last and p == N_PIECES - 1 and mb == N_MB - 1
                    c0 = 0
                    while c0 < PIECE:
                        width = max((PIECE - c0) // 2, TAIL_WIDTH) if final else PIECE
                        columns = slice(p * PIECE + c0, p * PIECE + c0 + width)
                        acc = psum.tile([P, width], F32, tag="bank")
                        for jb in range(N_JB):
                            nc.tensor.matmul(
                                acc[:],
                                uT[:, jb, mb * P : (mb + 1) * P],
                                adj_sb[p][:, jb, c0 : c0 + width],
                                start=(jb == 0),
                                stop=(jb == N_JB - 1),
                            )
                            flip = mb * N_JB + jb
                            if l == 0 and p == 0 and flip < FLIP_LAG * JB_IN_PIECE:
                                flip_block(len(units) - FLIP_LAG + flip // JB_IN_PIECE, flip % JB_IN_PIECE)
                        biased = stage.tile([P, width], F32, tag="biased")
                        nc.scalar.activation(biased[:], acc[:], IDENTITY, bias=bias_sb[l][:, mb, :])
                        if not last:
                            nc.vector.scalar_tensor_tensor(
                                h_bf[:, mb, columns], biased[:], ALPHA, biased[:], op0=MULT, op1=MAX
                            )
                        h = stage.tile([P, width], F32, tag="h")
                        nc.vector.scalar_tensor_tensor(h[:], biased[:], ALPHA, biased[:], op0=MULT, op1=MAX)
                        rows = slice(l * M + mb * P, l * M + (mb + 1) * P)
                        nc.sync.dma_start(out[rows, columns], h[:])
                        c0 += width

            if not last:
                uT = layer_pool.tile([P, N_JB, M], BF16, name="uT")
                for jb0 in range(0, N_JB, 2):
                    u_ps = psum.tile([P, 2, M], F32, tag="bank")
                    for k in range(2):
                        jb = jb0 + k
                        for fb in range(N_MB):
                            nc.tensor.matmul(
                                u_ps[:, k, :],
                                h_bf[:, fb, jb * P : (jb + 1) * P],
                                w_sb[l + 1][:, fb, :],
                                start=(fb == 0),
                                stop=(fb == N_MB - 1),
                            )
                    if (jb0 // 2) % 2 == 0:
                        nc.vector.tensor_copy(uT[:, jb0 : jb0 + 2, :], u_ps[:])
                    else:
                        nc.scalar.copy(uT[:, jb0 : jb0 + 2, :], u_ps[:])
